import numpy as np
import ml_dtypes


def mxq(x, axis, fmt="e4m3"):
    dtype, down = {"e4m3": (ml_dtypes.float8_e4m3fn, 7), "e5m2": (ml_dtypes.float8_e5m2, 14)}[fmt]
    v = np.moveaxis(np.asarray(x, np.float32).astype(ml_dtypes.bfloat16).astype(np.float64), axis, -1)
    blocks = v.reshape(v.shape[:-1] + (-1, 32))
    amax = np.abs(blocks).max(-1, keepdims=True)
    byte = np.maximum(np.where(amax > 0, np.frexp(amax)[1] - 1 + 127, 0) - down, 1)
    scale = np.exp2(byte - 127.0)
    codes = (blocks / scale).astype(np.float32).astype(dtype).astype(np.float64)
    return np.moveaxis((codes * scale).reshape(v.shape), -1, axis)


WIDE = False


def mx_kscale(k):
    if not WIDE:
        return np.ones(k)
    levels = np.array([30, -30])
    if k % 512:
        return np.exp2(np.random.permutation(np.resize(levels, k // 32))).repeat(32)
    a = np.empty((k // 512, 16))
    for p in range(k // 512):
        a[p, :8] = np.random.permutation(np.resize(levels, 8))
        for g in range(8):
            far = levels[np.abs(levels - a[p, g]) >= 10]
            a[p, g + 8] = far[np.random.randint(len(far))]
    return np.exp2(a.ravel()).repeat(32)


BF16 = ml_dtypes.bfloat16


def bf(x):
    return np.asarray(x, np.float32).astype(BF16)


def f64(x):
    return np.asarray(x).astype(np.float64)


B, T, C, H, G = 2, 512, 1024, 16, 16
HS = C // H
TG = T // G
THETA = 10000.0


def apply_rope(t, cos, sin):
    tp = t.reshape(B, T, H, HS // 2, 2)
    a, b = tp[..., 0], tp[..., 1]
    c = cos[None, :, None, :]
    s = sin[None, :, None, :]
    return np.stack([a * c - b * s, a * s + b * c], axis=-1).reshape(B, T, H, HS)


def grp(t):
    return t.reshape(B, G, TG, H, HS).transpose(0, 3, 1, 2, 4)


def with_summary(t):
    return np.concatenate([t, t.mean(axis=3, keepdims=True)], axis=3)


def setup_inputs():
    s = mx_kscale(C)
    x = np.random.standard_normal((B, T, C)) * 0.7 + np.random.standard_normal((B, 1, C)) * 0.7
    w = np.random.standard_normal((3 * C, C)) / np.sqrt(C)
    ang = np.arange(T)[:, None] / THETA ** (np.arange(0, HS, 2) / HS)[None, :]
    return {"x": bf(x * s), "w_attn": bf(w / s[None, :]), "freqs_cos": bf(np.cos(ang)), "freqs_sin": bf(np.sin(ang))}


def reference(x, w_attn, freqs_cos, freqs_sin):
    cos, sin = f64(freqs_cos), f64(freqs_sin)
    qkv = mxq(f64(x), 2, "e5m2") @ mxq(f64(w_attn), 1, "e5m2").T
    q, k, v = np.split(qkv, 3, axis=2)
    q = apply_rope(q.reshape(B, T, H, HS), cos, sin).reshape(B, T, C)
    k = apply_rope(k.reshape(B, T, H, HS), cos, sin).reshape(B, T, C)
    q, k, v = grp(q), grp(k), grp(v)
    return with_summary(q), with_summary(k), with_summary(v)

@@ -1,0 +1,337 @@
+from contextlib import ExitStack
+
+import concourse.masks as masks
+import concourse.mybir as mybir
+
+FLOPS = 2 * 1024 * 3072 * 1024
+
+F32 = mybir.dt.float32
+BF16 = mybir.dt.bfloat16
+U32 = mybir.dt.uint32
+U8 = mybir.dt.uint8
+FP8X4 = mybir.dt.float8_e5m2_x4
+ALU = mybir.AluOpType
+
+P = 128
+NB = 2
+RL = 4
+KP = 2
+HB = 8
+HS = 64
+UNITS = ((0, 0), (0, 1), (2, 0), (4, 0), (2, 1), (4, 1), (1, 0), (1, 1), (5, 0), (3, 0), (3, 1), (5, 1))
+DIRECT = (2, 3)
+MANUAL = True
+LIMIT_R = 2
+LIMIT_V = 1
+AHEAD = 12
+
+
+def tile_causalselfattention2_pa_kernel(tc, x, w_attn, freqs_cos, freqs_sin, out_0, out_1, out_2):
+    nc = tc.nc
+    outs = (out_0, out_1, out_2)
+
+    with ExitStack() as ctx:
+        const = ctx.enter_context(tc.tile_pool(name="const", bufs=1))
+        wraw = ctx.enter_context(tc.tile_pool(name="wraw", bufs=5))
+        stage = ctx.enter_context(tc.tile_pool(name="stage", bufs=3))
+        wq = ctx.enter_context(tc.tile_pool(name="wq", bufs=4))
+        opool = ctx.enter_context(tc.tile_pool(name="opool", bufs=6))
+        mpool = ctx.enter_context(tc.tile_pool(name="mpool", bufs=4))
+        work = ctx.enter_context(tc.tile_pool(name="work", bufs=2))
+        psum = ctx.enter_context(tc.psum_pool(name="psum", bufs=1))
+
+        blocks = []
+        for n, b in UNITS:
+            if n not in blocks:
+                blocks.append(n)
+
+        cos_sb = const.tile([P, RL, 32], BF16, name="cos_sb")
+        sin_sb = const.tile([P, RL, 32], BF16, name="sin_sb")
+        nc.scalar.dma_start(out=cos_sb[:], in_=freqs_cos.rearrange("(p j) i -> p j i", j=RL))
+        nc.scalar.dma_start(out=sin_sb[:], in_=freqs_sin.rearrange("(p j) i -> p j i", j=RL))
+
+        rows_of = {}
+        for j in range(RL):
+            rows_of[("x", 0, j)] = const.tile([P, 1024], BF16, name="x0_%d" % j)
+            rows_of[("w", blocks[0], j)] = const.tile([P, 1024], BF16, name="w0_%d" % j)
+        x1_sb = const.tile([P, RL, 1024], BF16, name="x1_sb")
+        for j in range(RL):
+            rows_of[("x", 1, j)] = x1_sb[:, j, :]
+        w_sb = {}
+        for n in blocks[1:]:
+            w_sb[n] = wraw.tile([P, 4, 1024], BF16, name="w_sb", tag="w_sb")
+            for t in range(4):
+                rows_of[("w", n, t)] = w_sb[n][:, t, :]
+
+        def w_rows(n):
+            return w_attn[512 * n : 512 * (n + 1), :].rearrange("(t p) k -> p t k", p=P)
+
+        for t in range(4):
+            nc.sync.dma_start(out=rows_of[("w", blocks[0], t)][:], in_=w_rows(blocks[0])[:, t, :])
+        x_rows = x.rearrange("b (p j) k -> b p j k", j=RL)
+        for j in range(RL):
+            nc.sync.dma_start(out=rows_of[("x", 0, j)][:], in_=x_rows[0, :, j, :])
+        nc.sync.dma_start(out=x1_sb[:], in_=x_rows[1])
+        for n in blocks[1:]:
+            nc.sync.dma_start(out=w_sb[n][:], in_=w_rows(n))
+
+        ident = const.tile([P, P], F32, name="ident")
+        masks.make_identity(nc, ident[:])
+        bdiag = const.tile([P, P], F32, name="bdiag")
+        masks.make_block_diagonal(nc, bdiag[:], 8)
+        gsel = const.tile([P, 16], F32, name="gsel")
+        nc.vector.tensor_copy(out=gsel[:], in_=bdiag[:, 0:P:8])
+        fold = const.tile([P, HS], F32, name="fold")
+        nc.vector.tensor_tensor(out=fold[:], in0=ident[:, 0:HS], in1=ident[:, HS:P], op=ALU.add)
+
+        ctab = const.tile([P, RL, HS], F32, name="ctab")
+        stab = const.tile([P, RL, HS], F32, name="stab")
+        nc.vector.tensor_copy(
+            out=ctab[:].rearrange("p j (i e) -> p j i e", e=2),
+            in_=cos_sb[:].unsqueeze(3).to_broadcast([P, RL, 32, 2]),
+        )
+        stab_v = stab[:].rearrange("p j (i e) -> p j i e", e=2)
+        nc.vector.tensor_scalar_mul(out=stab_v[:, :, :, 0], in0=sin_sb[:], scalar1=-1.0)
+        nc.vector.tensor_copy(out=stab_v[:, :, :, 1], in_=sin_sb[:])
+
+        xc = {}
+        xs = {}
+        for b in range(NB):
+            for j in range(RL):
+                xc[(b, j)] = const.tile([P, KP, P], U32, name="xc%d_%d" % (b, j), align_bytes=64)
+                xs[(b, j)] = const.tile([P, KP, P], U8, name="xs%d_%d" % (b, j), align_bytes=64)
+
+        if MANUAL:
+            ctx.enter_context(tc.manual_schedule())
+
+        state = {"step": 0}
+        prep_q = []
+        mean_q = []
+        vec_q = []
+        ready_ops = set()
+        grouped_of = {}
+        wcodes = {}
+
+        def quant(key, grouped, codes, scales, done):
+            def run():
+                for g in range(KP):
+                    nc.vector.quantize_mx(
+                        out=codes[:, g, :].bitcast(FP8X4),
+                        scales=scales[:, g, :],
+                        in_=grouped[:, g].rearrange("p t r j -> p (t r j)"),
+                    )
+                if done:
+                    ready_ops.add(key)
+
+            return run
+
+        def tile_prep(kind, idx, t, fine):
+            s = state["step"]
+            if kind == "w" and t == 0:
+                wc = wq.tile([P, KP, 512], U32, name="wc", tag="wc", align_bytes=64)
+                ws = wq.tile([P, KP, 512], U8, name="ws", tag="ws", align_bytes=64)
+                wcodes[idx] = (wc, ws)
+            single = kind == "x" or fine
+            if single:
+                grouped = stage.tile([P, KP, 1, P, 4], BF16, name="grouped1", tag="grouped1", bufs=4, align_bytes=64)
+                slot = 0
+            else:
+                if t == 0:
+                    grouped_of[idx] = stage.tile([P, KP, 4, P, 4], BF16, name="grouped", tag="grouped", align_bytes=64)
+                grouped = grouped_of[idx]
+                slot = t
+            words = rows_of[(kind, idx, t)].bitcast(F32)
+            tp = psum.tile([P, KP, 2, P], F32, name="tp", tag="tp", bufs=2)
+            for g in range(KP):
+                for u in range(2):
+                    nc.tensor.transpose(tp[:, g, u, :], words[:, 256 * g + u : 256 * (g + 1) : 2], ident[:])
+            nc.scalar.copy(out=grouped[:].bitcast(F32)[:, :, slot, :, :], in_=tp[:].rearrange("p g u r -> p g r u"))
+            if kind == "x":
+                vec_q.append([s + 1, ("x", idx, t), quant(("x", idx, t), grouped, xc[(idx, t)], xs[(idx, t)], True)])
+            elif fine:
+                cols = slice(P * t, P * (t + 1))
+                vec_q.append([s, ("w", idx), quant(("w", idx), grouped, wcodes[idx][0][:, :, cols], wcodes[idx][1][:, :, cols], t == 3)])
+            elif t == 3:
+                vec_q.append([s + 2, ("w", idx), quant(("w", idx), grouped, wcodes[idx][0], wcodes[idx][1], True)])
+
+        def prep_entry(ready, kind, idx, t):
+            return [ready, lambda: tile_prep(kind, idx, t, False)]
+
+        def run_vec(s):
+            while vec_q and vec_q[0][0] <= s:
+                vec_q.pop(0)[2]()
+
+        def ensure(key):
+            while key not in ready_ops:
+                if any(e[1] == key for e in vec_q):
+                    vec_q.pop(0)[2]()
+                else:
+                    prep_q.pop(0)[1]()
+
+        def fill(s, limit):
+            n_run = 0
+            while n_run < limit and prep_q and prep_q[0][0] <= s:
+                prep_q.pop(0)[1]()
+                n_run += 1
+            while n_run < limit and mean_q and mean_q[0][0] <= s:
+                mean_q.pop(0)[1]()
+                n_run += 1
+
+        def store_mean(n, b, t_ps):
+            which, hn = n // 2, n % 2
+            heads = slice(HB * hn, HB * (hn + 1))
+            if b is None:
+                mean_sb = work.tile([P, NB, HS], F32, name="mean_sb", tag="mean_sb")
+                nc.scalar.copy(out=mean_sb[:], in_=t_ps[:].rearrange("p (b d) -> p b d", b=NB))
+                nc.sync.dma_start(out=outs[which][:, heads, :, 32, :].rearrange("b h g d -> (h g) b d"), in_=mean_sb[:])
+            else:
+                mean_one = work.tile([P, HS], F32, name="mean_one", tag="mean_one")
+                nc.scalar.copy(out=mean_one[:], in_=t_ps[:])
+                nc.sync.dma_start(out=outs[which][b, heads, :, 32, :].rearrange("h g d -> (h g) d"), in_=mean_one[:])
+
+        def push_mean(ready, n, b, src):
+            hold = {}
+            parts = 1 if b is None else 2
+
+            def finish():
+                r_sb = hold["r_sb"]
+                if b is None:
+                    t_ps = psum.tile([P, P], F32, name="t_ps", tag="t_ps", bufs=1)
+                    nc.tensor.transpose(t_ps[:], r_sb[:], ident[:])
+                else:
+                    t_ps = psum.tile([P, HS], F32, name="t_ps", tag="t_ps", bufs=1)
+                    nc.tensor.matmul(out=t_ps[:], lhsT=r_sb[:], rhs=fold[:], start=True, stop=True)
+                store_mean(n, b, t_ps)
+
+            def chunk(h0, h1):
+                def run():
+                    if h0 == 0:
+                        hold["r_ps"] = psum.tile([P, HB, 16], F32, name="r_ps", tag="r_ps", bufs=1)
+                    r_ps = hold["r_ps"]
+                    for h in range(h0, h1):
+                        for a in range(parts):
+                            nc.tensor.matmul(
+                                out=r_ps[:, h, :],
+                                lhsT=src[:, h, 2 * a : 2 * a + 2, :].rearrange("p a d -> p (a d)"),
+                                rhs=gsel[:],
+                                start=(a == 0),
+                                stop=(a == parts - 1),
+                            )
+                    if h1 == HB:
+                        r_sb = work.tile([P, P], F32, name="r_sb", tag="r_sb")
+                        nc.scalar.mul(out=r_sb[:], in_=r_ps[:].rearrange("p h g -> p (h g)"), mul=1.0 / 32.0)
+                        hold["r_sb"] = r_sb
+                        mean_q[0:0] = [[state["step"] + 1, finish]]
+
+                return run
+
+            width = 4 // parts
+            for h0 in range(0, HB, width):
+                mean_q.append([ready, chunk(h0, h0 + width)])
+
+        sums = {}
+        seen = set()
+        live = {}
+
+        def step(k, j):
+            n, b = UNITS[k]
+            which, hn = n // 2, n % 2
+            rope = which < 2
+            s = RL * k + j
+            state["step"] = s
+            fill(s, LIMIT_R if rope else LIMIT_V)
+            ensure(("x", b, j))
+            ensure(("w", n))
+            wc, ws = wcodes[n]
+            if j == 0:
+                live["o"] = opool.tile([P, HB, RL, HS], F32, name="o", tag="o")
+                if n not in DIRECT and n not in sums:
+                    sums[n] = work.tile([P, HB, NB, HS], F32, name="gsum", tag="gsum")
+            o = live["o"]
+            ps = psum.tile([P, 512], F32, name="ps", tag="ps", bufs=4)
+            for g in range(KP):
+                nc.tensor.matmul_mx(
+                    out=ps[:],
+                    lhsT=xc[(b, j)][:, g, :].bitcast(FP8X4),
+                    lhsT_scale=xs[(b, j)][:, g, :],
+                    rhs=wc[:, g, :].bitcast(FP8X4),
+                    rhs_scale=ws[:, g, :],
+                    start=(g == 0),
+                    stop=(g == KP - 1),
+                )
+            ps_hd = ps[:].rearrange("p (h d) -> p h d", h=HB)
+            if rope:
+                if j % 2 == 0:
+                    live["m1"] = mpool.tile([P, HB, 2, HS], F32, name="m1", tag="m1")
+                    live["m2"] = mpool.tile([P, HB, 2, HS], F32, name="m2", tag="m2")
+                m1 = live["m1"]
+                m2 = live["m2"]
+                nc.vector.tensor_tensor(
+                    out=m1[:, :, j % 2, :],
+                    in0=ps_hd,
+                    in1=ctab[:, j, :].unsqueeze(1).to_broadcast([P, HB, HS]),
+                    op=ALU.mult,
+                )
+                nc.vector.tensor_tensor(
+                    out=m2[:, :, j % 2, :].rearrange("p h (i e) -> p h i e", e=2),
+                    in0=ps[:].rearrange("p (h i e) -> p h i e", h=HB, e=2)[:, :, :, ::-1],
+                    in1=stab[:, j, :].rearrange("p (i e) -> p i e", e=2).unsqueeze(1).to_broadcast([P, HB, 32, 2]),
+                    op=ALU.mult,
+                )
+                if j % 2 == 1:
+                    nc.gpsimd.tensor_tensor(
+                        out=o[:, :, j - 1 : j + 1, :],
+                        in0=m1[:],
+                        in1=m2[:],
+                        op=ALU.add,
+                    )
+            else:
+                nc.scalar.copy(out=o[:, :, j, :], in_=ps_hd)
+                if n not in DIRECT and j == 0:
+                    live["acc"] = work.tile([P, HB, HS], F32, name="acc", tag="acc", bufs=3)
+                    nc.scalar.copy(out=live["acc"][:], in_=ps_hd)
+                if n not in DIRECT and j > 0:
+                    prev = live["acc"][:]
+                    if j < RL - 1:
+                        live["acc"] = work.tile([P, HB, HS], F32, name="acc", tag="acc", bufs=3)
+                        dst = live["acc"][:]
+                    else:
+                        dst = sums[n][:, :, b, :]
+                    nc.vector.tensor_tensor(out=dst, in0=ps_hd, in1=prev, op=ALU.add)
+            run_vec(s)
+            if j < RL - 1:
+                return
+            if rope and n not in DIRECT:
+                half = work.tile([P, HB, 2, HS], F32, name="half", tag="half")
+                nc.gpsimd.tensor_tensor(out=half[:], in0=o[:, :, 0:2, :], in1=o[:, :, 2:4, :], op=ALU.add)
+                nc.gpsimd.tensor_tensor(out=sums[n][:, :, b, :], in0=half[:, :, 0, :], in1=half[:, :, 1, :], op=ALU.add)
+            for h in range(HB):
+                nc.sync.dma_start(
+                    out=outs[which][b, HB * hn + h, :, 0:32, :].rearrange("g (rh rl) d -> g rh (rl d)", rl=RL),
+                    in_=o[:, h, :, :].rearrange("p rl d -> p (rl d)"),
+                )
+            if n in DIRECT:
+                push_mean(s + (6 if rope else 2), n, b, o)
+            elif n in seen:
+                push_mean(s + (8 if rope else 2), n, None, sums[n])
+            seen.add(n)
+
+        for t in range(4):
+            tile_prep("w", blocks[0], t, True)
+            run_vec(0)
+        tile_prep("x", 0, 0, False)
+        tile_prep("x", 0, 1, False)
+        for t in (2, 3):
+            prep_q.append(prep_entry(0, "x", 0, t))
+        for t in range(4):
+            prep_q.append(prep_entry(0, "x", 1, t))
+        for n in blocks[1:]:
+            need = RL * min(k for k in range(len(UNITS)) if UNITS[k][0] == n)
+            for t in range(4):
+                prep_q.append(prep_entry(max(0, need - AHEAD), "w", n, t))
+
+        for k in range(len(UNITS)):
+            for j in range(RL):
+                step(k, j)
+        while mean_q:
+            mean_q.pop(0)[1]()

@@ -11,6 +11,7 @@ U32 = mybir.dt.uint32
 U8 = mybir.dt.uint8
 FP8X4 = mybir.dt.float8_e5m2_x4
 ALU = mybir.AluOpType
+AX = mybir.AxisListType
 
 P = 128
 NB = 2
@@ -18,12 +19,13 @@ RL = 4
 KP = 2
 HB = 8
 HS = 64
-UNITS = ((0, 0), (0, 1), (2, 0), (4, 0), (2, 1), (4, 1), (1, 0), (1, 1), (5, 0), (3, 0), (3, 1), (5, 1))
-DIRECT = (2, 3)
-MANUAL = True
-LIMIT_R = 2
-LIMIT_V = 1
-AHEAD = 12
+UNITS = ((0, 0), (0, 1), (4, 0), (2, 0), (2, 1), (4, 1), (1, 0), (1, 1), (5, 0), (3, 0), (3, 1), (5, 1))
+VTREE = ((2, 0), (1, 0), (3, 0))
+MANUAL = False
+SLOTS = (0, 1, 2, 3)
+AHEAD = 7
+GLAG = 4
+MLAG = 8
 
 
 def tile_causalselfattention2_pa_kernel(tc, x, w_attn, freqs_cos, freqs_sin, out_0, out_1, out_2):
@@ -35,7 +37,7 @@ def tile_causalselfattention2_pa_kernel(tc, x, w_attn, freqs_cos, freqs_sin, out
         wraw = ctx.enter_context(tc.tile_pool(name="wraw", bufs=5))
         stage = ctx.enter_context(tc.tile_pool(name="stage", bufs=3))
         wq = ctx.enter_context(tc.tile_pool(name="wq", bufs=4))
-        opool = ctx.enter_context(tc.tile_pool(name="opool", bufs=6))
+        opool = ctx.enter_context(tc.tile_pool(name="opool", bufs=5))
         mpool = ctx.enter_context(tc.tile_pool(name="mpool", bufs=4))
         work = ctx.enter_context(tc.tile_pool(name="work", bufs=2))
         psum = ctx.enter_context(tc.psum_pool(name="psum", bufs=1))
@@ -79,10 +81,6 @@ def tile_causalselfattention2_pa_kernel(tc, x, w_attn, freqs_cos, freqs_sin, out
         masks.make_identity(nc, ident[:])
         bdiag = const.tile([P, P], F32, name="bdiag")
         masks.make_block_diagonal(nc, bdiag[:], 8)
-        gsel = const.tile([P, 16], F32, name="gsel")
-        nc.vector.tensor_copy(out=gsel[:], in_=bdiag[:, 0:P:8])
-        fold = const.tile([P, HS], F32, name="fold")
-        nc.vector.tensor_tensor(out=fold[:], in0=ident[:, 0:HS], in1=ident[:, HS:P], op=ALU.add)
 
         ctab = const.tile([P, RL, HS], F32, name="ctab")
         stab = const.tile([P, RL, HS], F32, name="stab")
@@ -96,10 +94,13 @@ def tile_causalselfattention2_pa_kernel(tc, x, w_attn, freqs_cos, freqs_sin, out
 
         xc = {}
         xs = {}
-        for b in range(NB):
-            for j in range(RL):
-                xc[(b, j)] = const.tile([P, KP, P], U32, name="xc%d_%d" % (b, j), align_bytes=64)
-                xs[(b, j)] = const.tile([P, KP, P], U8, name="xs%d_%d" % (b, j), align_bytes=64)
+        xc1 = const.tile([P, KP, 512], U32, name="xc1", align_bytes=64)
+        xs1 = const.tile([P, KP, 512], U8, name="xs1", align_bytes=64)
+        for j in range(RL):
+            xc[(0, j)] = const.tile([P, KP, P], U32, name="xc0_%d" % j, align_bytes=64)
+            xs[(0, j)] = const.tile([P, KP, P], U8, name="xs0_%d" % j, align_bytes=64)
+            xc[(1, j)] = xc1[:, :, P * j : P * (j + 1)]
+            xs[(1, j)] = xs1[:, :, P * j : P * (j + 1)]
 
         if MANUAL:
             ctx.enter_context(tc.manual_schedule())
@@ -120,8 +121,8 @@ def tile_causalselfattention2_pa_kernel(tc, x, w_attn, freqs_cos, freqs_sin, out
                         scales=scales[:, g, :],
                         in_=grouped[:, g].rearrange("p t r j -> p (t r j)"),
                     )
-                if done:
-                    ready_ops.add(key)
+                for one in done:
+                    ready_ops.add(one)
 
             return run
 
@@ -131,14 +132,14 @@ def tile_causalselfattention2_pa_kernel(tc, x, w_attn, freqs_cos, freqs_sin, out
                 wc = wq.tile([P, KP, 512], U32, name="wc", tag="wc", align_bytes=64)
                 ws = wq.tile([P, KP, 512], U8, name="ws", tag="ws", align_bytes=64)
                 wcodes[idx] = (wc, ws)
-            single = kind == "x" or fine
+            single = fine or (kind == "x" and idx == 0)
             if single:
                 grouped = stage.tile([P, KP, 1, P, 4], BF16, name="grouped1", tag="grouped1", bufs=4, align_bytes=64)
                 slot = 0
             else:
                 if t == 0:
-                    grouped_of[idx] = stage.tile([P, KP, 4, P, 4], BF16, name="grouped", tag="grouped", align_bytes=64)
-                grouped = grouped_of[idx]
+                    grouped_of[(kind, idx)] = stage.tile([P, KP, 4, P, 4], BF16, name="grouped", tag="grouped", align_bytes=64)
+                grouped = grouped_of[(kind, idx)]
                 slot = t
             words = rows_of[(kind, idx, t)].bitcast(F32)
             tp = psum.tile([P, KP, 2, P], F32, name="tp", tag="tp", bufs=2)
@@ -146,16 +147,23 @@ def tile_causalselfattention2_pa_kernel(tc, x, w_attn, freqs_cos, freqs_sin, out
                 for u in range(2):
                     nc.tensor.transpose(tp[:, g, u, :], words[:, 256 * g + u : 256 * (g + 1) : 2], ident[:])
             nc.scalar.copy(out=grouped[:].bitcast(F32)[:, :, slot, :, :], in_=tp[:].rearrange("p g u r -> p g r u"))
-            if kind == "x":
-                vec_q.append([s + 1, ("x", idx, t), quant(("x", idx, t), grouped, xc[(idx, t)], xs[(idx, t)], True)])
+            if kind == "x" and idx == 0:
+                vec_q.append([s + 1, ("x", 0, t), quant(("x", 0, t), grouped, xc[(0, t)], xs[(0, t)], [("x", 0, t)])])
             elif fine:
                 cols = slice(P * t, P * (t + 1))
-                vec_q.append([s, ("w", idx), quant(("w", idx), grouped, wcodes[idx][0][:, :, cols], wcodes[idx][1][:, :, cols], t == 3)])
+                done = [("w", idx)] if t == 3 else []
+                vec_q.append([s, ("w", idx), quant(("w", idx), grouped, wcodes[idx][0][:, :, cols], wcodes[idx][1][:, :, cols], done)])
+            elif t == 3 and kind == "x":
+                vec_q.append([s + 1, ("x", 1, 0), quant(("x", 1, 0), grouped, xc1, xs1, [("x", 1, jj) for jj in range(RL)])])
             elif t == 3:
-                vec_q.append([s + 2, ("w", idx), quant(("w", idx), grouped, wcodes[idx][0], wcodes[idx][1], True)])
+                vec_q.append([s + 2, ("w", idx), quant(("w", idx), grouped, wcodes[idx][0], wcodes[idx][1], [("w", idx)])])
 
-        def prep_entry(ready, kind, idx, t):
-            return [ready, lambda: tile_prep(kind, idx, t, False)]
+        def prep_run(kind, idx, tiles):
+            def run():
+                for t in tiles:
+                    tile_prep(kind, idx, t, False)
+
+            return run
 
         def run_vec(s):
             while vec_q and vec_q[0][0] <= s:
@@ -168,70 +176,36 @@ def tile_causalselfattention2_pa_kernel(tc, x, w_attn, freqs_cos, freqs_sin, out
                 else:
                     prep_q.pop(0)[1]()
 
-        def fill(s, limit):
-            n_run = 0
-            while n_run < limit and prep_q and prep_q[0][0] <= s:
+        def fill(s):
+            if prep_q and prep_q[0][0] <= s:
                 prep_q.pop(0)[1]()
-                n_run += 1
-            while n_run < limit and mean_q and mean_q[0][0] <= s:
+            elif mean_q and mean_q[0][0] <= s:
                 mean_q.pop(0)[1]()
-                n_run += 1
 
-        def store_mean(n, b, t_ps):
+        def push_mean(ready, n, b, gsum):
             which, hn = n // 2, n % 2
-            heads = slice(HB * hn, HB * (hn + 1))
-            if b is None:
-                mean_sb = work.tile([P, NB, HS], F32, name="mean_sb", tag="mean_sb")
-                nc.scalar.copy(out=mean_sb[:], in_=t_ps[:].rearrange("p (b d) -> p b d", b=NB))
-                nc.sync.dma_start(out=outs[which][:, heads, :, 32, :].rearrange("b h g d -> (h g) b d"), in_=mean_sb[:])
-            else:
-                mean_one = work.tile([P, HS], F32, name="mean_one", tag="mean_one")
-                nc.scalar.copy(out=mean_one[:], in_=t_ps[:])
-                nc.sync.dma_start(out=outs[which][b, heads, :, 32, :].rearrange("h g d -> (h g) d"), in_=mean_one[:])
 
-        def push_mean(ready, n, b, src):
-            hold = {}
-            parts = 1 if b is None else 2
+            def run():
+                m_ps = psum.tile([P, 512], F32, name="m_ps", tag="m_ps", bufs=2)
+                nc.tensor.matmul(out=m_ps[:], lhsT=bdiag[:], rhs=gsum[:].rearrange("p h d -> p (h d)"), start=True, stop=True)
+                mean_sb = work.tile([P, HB, HS], F32, name="mean_sb", tag="mean_sb")
+                nc.scalar.mul(out=mean_sb[:].rearrange("p h d -> p (h d)"), in_=m_ps[:], mul=1.0 / 32.0)
+                nc.sync.dma_start(
+                    out=outs[which][b, HB * hn : HB * (hn + 1), :, 32, :].rearrange("h g d -> g h d"),
+                    in_=mean_sb[0:P:8, :, :],
+                )
 
-            def finish():
-                r_sb = hold["r_sb"]
-                if b is None:
-                    t_ps = psum.tile([P, P], F32, name="t_ps", tag="t_ps", bufs=1)
-                    nc.tensor.transpose(t_ps[:], r_sb[:], ident[:])
-                else:
-                    t_ps = psum.tile([P, HS], F32, name="t_ps", tag="t_ps", bufs=1)
-                    nc.tensor.matmul(out=t_ps[:], lhsT=r_sb[:], rhs=fold[:], start=True, stop=True)
-                store_mean(n, b, t_ps)
+            mean_q.append([ready, run])
 
-            def chunk(h0, h1):
-                def run():
-                    if h0 == 0:
-                        hold["r_ps"] = psum.tile([P, HB, 16], F32, name="r_ps", tag="r_ps", bufs=1)
-                    r_ps = hold["r_ps"]
-                    for h in range(h0, h1):
-                        for a in range(parts):
-                            nc.tensor.matmul(
-                                out=r_ps[:, h, :],
-                                lhsT=src[:, h, 2 * a : 2 * a + 2, :].rearrange("p a d -> p (a d)"),
-                                rhs=gsel[:],
-                                start=(a == 0),
-                                stop=(a == parts - 1),
-                            )
-                    if h1 == HB:
-                        r_sb = work.tile([P, P], F32, name="r_sb", tag="r_sb")
-                        nc.scalar.mul(out=r_sb[:], in_=r_ps[:].rearrange("p h g -> p (h g)"), mul=1.0 / 32.0)
-                        hold["r_sb"] = r_sb
-                        mean_q[0:0] = [[state["step"] + 1, finish]]
-
-                return run
-
-            width = 4 // parts
-            for h0 in range(0, HB, width):
-                mean_q.append([ready, chunk(h0, h0 + width)])
-
-        sums = {}
-        seen = set()
         live = {}
+        tree_q = []
+
+        def vector_tree(n, b, o, gsum):
+            def run():
+                nc.vector.tensor_reduce(out=gsum[:], in_=o[:].rearrange("p h r d -> p h d r"), axis=AX.X, op=ALU.add)
+                push_mean(state["step"] + 1, n, b, gsum)
+
+            return run
 
         def step(k, j):
             n, b = UNITS[k]
@@ -239,15 +213,14 @@ def tile_causalselfattention2_pa_kernel(tc, x, w_attn, freqs_cos, freqs_sin, out
             rope = which < 2
             s = RL * k + j
             state["step"] = s
-            fill(s, LIMIT_R if rope else LIMIT_V)
             ensure(("x", b, j))
             ensure(("w", n))
             wc, ws = wcodes[n]
             if j == 0:
                 live["o"] = opool.tile([P, HB, RL, HS], F32, name="o", tag="o")
-                if n not in DIRECT and n not in sums:
-                    sums[n] = work.tile([P, HB, NB, HS], F32, name="gsum", tag="gsum")
+                live["gsum"] = work.tile([P, HB, HS], F32, name="gsum", tag="gsum", bufs=4)
             o = live["o"]
+            gsum = live["gsum"]
             ps = psum.tile([P, 512], F32, name="ps", tag="ps", bufs=4)
             for g in range(KP):
                 nc.tensor.matmul_mx(
@@ -259,6 +232,8 @@ def tile_causalselfattention2_pa_kernel(tc, x, w_attn, freqs_cos, freqs_sin, out
                     start=(g == 0),
                     stop=(g == KP - 1),
                 )
+            if rope and j in SLOTS:
+                fill(s)
             ps_hd = ps[:].rearrange("p (h d) -> p h d", h=HB)
             if rope:
                 if j % 2 == 0:
@@ -279,59 +254,56 @@ def tile_causalselfattention2_pa_kernel(tc, x, w_attn, freqs_cos, freqs_sin, out
                     op=ALU.mult,
                 )
                 if j % 2 == 1:
-                    nc.gpsimd.tensor_tensor(
-                        out=o[:, :, j - 1 : j + 1, :],
-                        in0=m1[:],
-                        in1=m2[:],
-                        op=ALU.add,
-                    )
+                    nc.gpsimd.tensor_tensor(out=o[:, :, j - 1 : j + 1, :], in0=m1[:], in1=m2[:], op=ALU.add)
             else:
                 nc.scalar.copy(out=o[:, :, j, :], in_=ps_hd)
-                if n not in DIRECT and j == 0:
+                if j == 0:
                     live["acc"] = work.tile([P, HB, HS], F32, name="acc", tag="acc", bufs=3)
                     nc.scalar.copy(out=live["acc"][:], in_=ps_hd)
-                if n not in DIRECT and j > 0:
+                else:
                     prev = live["acc"][:]
                     if j < RL - 1:
                         live["acc"] = work.tile([P, HB, HS], F32, name="acc", tag="acc", bufs=3)
                         dst = live["acc"][:]
                     else:
-                        dst = sums[n][:, :, b, :]
+                        dst = gsum[:]
                     nc.vector.tensor_tensor(out=dst, in0=ps_hd, in1=prev, op=ALU.add)
             run_vec(s)
+            while tree_q and tree_q[0][0] <= s:
+                tree_q.pop(0)[1]()
             if j < RL - 1:
                 return
-            if rope and n not in DIRECT:
+            if rope and (n, b) not in VTREE:
                 half = work.tile([P, HB, 2, HS], F32, name="half", tag="half")
                 nc.gpsimd.tensor_tensor(out=half[:], in0=o[:, :, 0:2, :], in1=o[:, :, 2:4, :], op=ALU.add)
-                nc.gpsimd.tensor_tensor(out=sums[n][:, :, b, :], in0=half[:, :, 0, :], in1=half[:, :, 1, :], op=ALU.add)
+                nc.gpsimd.tensor_tensor(out=gsum[:], in0=half[:, :, 0, :], in1=half[:, :, 1, :], op=ALU.add)
             for h in range(HB):
                 nc.sync.dma_start(
                     out=outs[which][b, HB * hn + h, :, 0:32, :].rearrange("g (rh rl) d -> g rh (rl d)", rl=RL),
                     in_=o[:, h, :, :].rearrange("p rl d -> p (rl d)"),
                 )
-            if n in DIRECT:
-                push_mean(s + (6 if rope else 2), n, b, o)
-            elif n in seen:
-                push_mean(s + (8 if rope else 2), n, None, sums[n])
-            seen.add(n)
+            if rope and (n, b) in VTREE:
+                tree_q.append([s + GLAG, vector_tree(n, b, o, gsum)])
+            else:
+                push_mean(s + (MLAG if rope else 1), n, b, gsum)
 
         for t in range(4):
             tile_prep("w", blocks[0], t, True)
             run_vec(0)
         tile_prep("x", 0, 0, False)
         tile_prep("x", 0, 1, False)
-        for t in (2, 3):
-            prep_q.append(prep_entry(0, "x", 0, t))
-        for t in range(4):
-            prep_q.append(prep_entry(0, "x", 1, t))
+        prep_q.append([0, prep_run("x", 0, (2,))])
+        prep_q.append([0, prep_run("x", 0, (3,))])
+        prep_q.append([0, prep_run("x", 1, (0, 1, 2, 3))])
         for n in blocks[1:]:
             need = RL * min(k for k in range(len(UNITS)) if UNITS[k][0] == n)
-            for t in range(4):
-                prep_q.append(prep_entry(max(0, need - AHEAD), "w", n, t))
+            prep_q.append([max(0, need - AHEAD), prep_run("w", n, (0, 1, 2, 3))])
 
         for k in range(len(UNITS)):
             for j in range(RL):
                 step(k, j)
-        while mean_q:
-            mean_q.pop(0)[1]()
+        while tree_q or mean_q:
+            if tree_q:
+                tree_q.pop(0)[1]()
+            else:
+                mean_q.pop(0)[1]()

@@ -26,6 +26,7 @@ SLOTS = (0, 1, 2, 3)
 AHEAD = 7
 GLAG = 4
 MLAG = 8
+PRECOPY = False
 
 
 def tile_causalselfattention2_pa_kernel(tc, x, w_attn, freqs_cos, freqs_sin, out_0, out_1, out_2):
@@ -113,9 +114,15 @@ def tile_causalselfattention2_pa_kernel(tc, x, w_attn, freqs_cos, freqs_sin, out
         grouped_of = {}
         wcodes = {}
 
-        def quant(key, grouped, codes, scales, done):
+        def quant(key, grouped, codes, scales, done, merged=True):
             def run():
-                for g in range(KP):
+                if merged:
+                    nc.vector.quantize_mx(
+                        out=codes[:].rearrange("p g c -> p (g c)").bitcast(FP8X4),
+                        scales=scales[:].rearrange("p g c -> p (g c)"),
+                        in_=grouped[:].rearrange("p g t r j -> p (g t r j)"),
+                    )
+                for g in range(0 if merged else KP):
                     nc.vector.quantize_mx(
                         out=codes[:, g, :].bitcast(FP8X4),
                         scales=scales[:, g, :],
@@ -143,16 +150,22 @@ def tile_causalselfattention2_pa_kernel(tc, x, w_attn, freqs_cos, freqs_sin, out
                 slot = t
             words = rows_of[(kind, idx, t)].bitcast(F32)
             tp = psum.tile([P, KP, 2, P], F32, name="tp", tag="tp", bufs=2)
+            if PRECOPY and not single:
+                pre = stage.tile([P, KP, 2, P], F32, name="pre", tag="pre", bufs=4)
+                nc.scalar.copy(out=pre[:], in_=words.rearrange("p (g q u) -> p g u q", g=KP, u=2))
             for g in range(KP):
                 for u in range(2):
-                    nc.tensor.transpose(tp[:, g, u, :], words[:, 256 * g + u : 256 * (g + 1) : 2], ident[:])
+                    if PRECOPY and not single:
+                        nc.tensor.transpose(tp[:, g, u, :], pre[:, g, u, :], ident[:])
+                    else:
+                        nc.tensor.transpose(tp[:, g, u, :], words[:, 256 * g + u : 256 * (g + 1) : 2], ident[:])
             nc.scalar.copy(out=grouped[:].bitcast(F32)[:, :, slot, :, :], in_=tp[:].rearrange("p g u r -> p g r u"))
             if kind == "x" and idx == 0:
                 vec_q.append([s + 1, ("x", 0, t), quant(("x", 0, t), grouped, xc[(0, t)], xs[(0, t)], [("x", 0, t)])])
             elif fine:
                 cols = slice(P * t, P * (t + 1))
                 done = [("w", idx)] if t == 3 else []
-                vec_q.append([s, ("w", idx), quant(("w", idx), grouped, wcodes[idx][0][:, :, cols], wcodes[idx][1][:, :, cols], done)])
+                vec_q.append([s, ("w", idx), quant(("w", idx), grouped, wcodes[idx][0][:, :, cols], wcodes[idx][1][:, :, cols], done, False)])
             elif t == 3 and kind == "x":
                 vec_q.append([s + 1, ("x", 1, 0), quant(("x", 1, 0), grouped, xc1, xs1, [("x", 1, jj) for jj in range(RL)])])
             elif t == 3:
@@ -253,7 +266,9 @@ def tile_causalselfattention2_pa_kernel(tc, x, w_attn, freqs_cos, freqs_sin, out
                     in1=stab[:, j, :].rearrange("p (i e) -> p i e", e=2).unsqueeze(1).to_broadcast([P, HB, 32, 2]),
                     op=ALU.mult,
                 )
-                if j % 2 == 1:
+                if k == 0:
+                    nc.gpsimd.tensor_tensor(out=o[:, :, j, :], in0=m1[:, :, j % 2, :], in1=m2[:, :, j % 2, :], op=ALU.add)
+                elif j % 2 == 1:
                     nc.gpsimd.tensor_tensor(out=o[:, :, j - 1 : j + 1, :], in0=m1[:], in1=m2[:], op=ALU.add)
             else:
                 nc.scalar.copy(out=o[:, :, j, :], in_=ps_hd)

@@ -19,14 +19,14 @@ RL = 4
 KP = 2
 HB = 8
 HS = 64
-UNITS = ((0, 0), (0, 1), (4, 0), (2, 0), (2, 1), (4, 1), (1, 0), (1, 1), (5, 0), (3, 0), (3, 1), (5, 1))
-VTREE = ((2, 0), (1, 0), (3, 0))
-MANUAL = False
-SLOTS = (0, 1, 2, 3)
-AHEAD = 7
-GLAG = 4
-MLAG = 8
-PRECOPY = False
+GP = 8
+
+UNITS = ((0, 0), (0, 1), (4, 0), (2, 0), (2, 1), (4, 1), (1, 0), (1, 1), (3, 0), (3, 1), (5, 0), (5, 1))
+VECTOR_SUMS = ((2, 0), (1, 0), (3, 0))
+PREP_AHEAD = 7
+QUANT_BEHIND = 2
+VECTOR_SUM_BEHIND = 4
+MEAN_BEHIND = 8
 
 
 def tile_causalselfattention2_pa_kernel(tc, x, w_attn, freqs_cos, freqs_sin, out_0, out_1, out_2):
@@ -80,8 +80,8 @@ def tile_causalselfattention2_pa_kernel(tc, x, w_attn, freqs_cos, freqs_sin, out
 
         ident = const.tile([P, P], F32, name="ident")
         masks.make_identity(nc, ident[:])
-        bdiag = const.tile([P, P], F32, name="bdiag")
-        masks.make_block_diagonal(nc, bdiag[:], 8)
+        same_group = const.tile([P, P], F32, name="bdiag")
+        masks.make_block_diagonal(nc, same_group[:], GP)
 
         ctab = const.tile([P, RL, HS], F32, name="ctab")
         stab = const.tile([P, RL, HS], F32, name="stab")
@@ -102,132 +102,106 @@ def tile_causalselfattention2_pa_kernel(tc, x, w_attn, freqs_cos, freqs_sin, out
             xs[(0, j)] = const.tile([P, KP, P], U8, name="xs0_%d" % j, align_bytes=64)
             xc[(1, j)] = xc1[:, :, P * j : P * (j + 1)]
             xs[(1, j)] = xs1[:, :, P * j : P * (j + 1)]
-
-        if MANUAL:
-            ctx.enter_context(tc.manual_schedule())
-
-        state = {"step": 0}
-        prep_q = []
-        mean_q = []
-        vec_q = []
-        ready_ops = set()
-        grouped_of = {}
         wcodes = {}
 
-        def quant(key, grouped, codes, scales, done, merged=True):
-            def run():
-                if merged:
-                    nc.vector.quantize_mx(
-                        out=codes[:].rearrange("p g c -> p (g c)").bitcast(FP8X4),
-                        scales=scales[:].rearrange("p g c -> p (g c)"),
-                        in_=grouped[:].rearrange("p g t r j -> p (g t r j)"),
-                    )
-                for g in range(0 if merged else KP):
-                    nc.vector.quantize_mx(
-                        out=codes[:, g, :].bitcast(FP8X4),
-                        scales=scales[:, g, :],
-                        in_=grouped[:, g].rearrange("p t r j -> p (t r j)"),
-                    )
-                for one in done:
-                    ready_ops.add(one)
+        prep_q = []
+        mean_q = []
+        quant_q = []
+        sum_q = []
+        quantised = set()
 
-            return run
+        def quantise(grouped, codes, scales):
+            nc.vector.quantize_mx(
+                out=codes[:].rearrange("p g c -> p (g c)").bitcast(FP8X4),
+                scales=scales[:].rearrange("p g c -> p (g c)"),
+                in_=grouped[:].rearrange("p g t r j -> p (g t r j)"),
+            )
 
-        def tile_prep(kind, idx, t, fine):
-            s = state["step"]
-            if kind == "w" and t == 0:
-                wc = wq.tile([P, KP, 512], U32, name="wc", tag="wc", align_bytes=64)
-                ws = wq.tile([P, KP, 512], U8, name="ws", tag="ws", align_bytes=64)
-                wcodes[idx] = (wc, ws)
-            single = fine or (kind == "x" and idx == 0)
-            if single:
-                grouped = stage.tile([P, KP, 1, P, 4], BF16, name="grouped1", tag="grouped1", bufs=4, align_bytes=64)
-                slot = 0
-            else:
-                if t == 0:
-                    grouped_of[(kind, idx)] = stage.tile([P, KP, 4, P, 4], BF16, name="grouped", tag="grouped", align_bytes=64)
-                grouped = grouped_of[(kind, idx)]
-                slot = t
-            words = rows_of[(kind, idx, t)].bitcast(F32)
+        def quantise_columns(grouped, codes, scales):
+            for g in range(KP):
+                nc.vector.quantize_mx(
+                    out=codes[:, g, :].bitcast(FP8X4),
+                    scales=scales[:, g, :],
+                    in_=grouped[:, g].rearrange("p t r j -> p (t r j)"),
+                )
+
+        def transpose_rows(rows, grouped, slot):
+            words = rows.bitcast(F32)
             tp = psum.tile([P, KP, 2, P], F32, name="tp", tag="tp", bufs=2)
-            if PRECOPY and not single:
-                pre = stage.tile([P, KP, 2, P], F32, name="pre", tag="pre", bufs=4)
-                nc.scalar.copy(out=pre[:], in_=words.rearrange("p (g q u) -> p g u q", g=KP, u=2))
             for g in range(KP):
                 for u in range(2):
-                    if PRECOPY and not single:
-                        nc.tensor.transpose(tp[:, g, u, :], pre[:, g, u, :], ident[:])
-                    else:
-                        nc.tensor.transpose(tp[:, g, u, :], words[:, 256 * g + u : 256 * (g + 1) : 2], ident[:])
+                    nc.tensor.transpose(tp[:, g, u, :], words[:, 256 * g + u : 256 * (g + 1) : 2], ident[:])
             nc.scalar.copy(out=grouped[:].bitcast(F32)[:, :, slot, :, :], in_=tp[:].rearrange("p g u r -> p g r u"))
-            if kind == "x" and idx == 0:
-                vec_q.append([s + 1, ("x", 0, t), quant(("x", 0, t), grouped, xc[(0, t)], xs[(0, t)], [("x", 0, t)])])
-            elif fine:
+
+        def new_w_codes(n):
+            wc = wq.tile([P, KP, 512], U32, name="wc", tag="wc", align_bytes=64)
+            ws = wq.tile([P, KP, 512], U8, name="ws", tag="ws", align_bytes=64)
+            wcodes[n] = (wc, ws)
+
+        def prepare_tile(operand, index, t, step):
+            if operand == "w" and t == 0:
+                new_w_codes(index)
+            grouped = stage.tile([P, KP, 1, P, 4], BF16, name="grouped1", tag="grouped1", bufs=4, align_bytes=64)
+            transpose_rows(rows_of[(operand, index, t)], grouped, 0)
+            if operand == "x":
+                quant_q.append([step + 1, [("x", 0, t)], lambda: quantise(grouped, xc[(0, t)], xs[(0, t)])])
+            else:
                 cols = slice(P * t, P * (t + 1))
-                done = [("w", idx)] if t == 3 else []
-                vec_q.append([s, ("w", idx), quant(("w", idx), grouped, wcodes[idx][0][:, :, cols], wcodes[idx][1][:, :, cols], done, False)])
-            elif t == 3 and kind == "x":
-                vec_q.append([s + 1, ("x", 1, 0), quant(("x", 1, 0), grouped, xc1, xs1, [("x", 1, jj) for jj in range(RL)])])
-            elif t == 3:
-                vec_q.append([s + 2, ("w", idx), quant(("w", idx), grouped, wcodes[idx][0], wcodes[idx][1], [("w", idx)])])
+                wc, ws = wcodes[index]
+                done = [("w", index)] if t == 3 else []
+                quant_q.append([step, done, lambda: quantise_columns(grouped, wc[:, :, cols], ws[:, :, cols])])
 
-        def prep_run(kind, idx, tiles):
-            def run():
-                for t in tiles:
-                    tile_prep(kind, idx, t, False)
+        def prepare_block(operand, index, step):
+            if operand == "w":
+                new_w_codes(index)
+            grouped = stage.tile([P, KP, 4, P, 4], BF16, name="grouped", tag="grouped", align_bytes=64)
+            for t in range(4):
+                transpose_rows(rows_of[(operand, index, t)], grouped, t)
+            if operand == "x":
+                quant_q.append([step + 1, [("x", 1, j) for j in range(RL)], lambda: quantise(grouped, xc1, xs1)])
+            else:
+                wc, ws = wcodes[index]
+                quant_q.append([step + QUANT_BEHIND, [("w", index)], lambda: quantise(grouped, wc, ws)])
 
-            return run
+        def write_quantiser():
+            entry = quant_q.pop(0)
+            entry[2]()
+            for operand in entry[1]:
+                quantised.add(operand)
 
-        def run_vec(s):
-            while vec_q and vec_q[0][0] <= s:
-                vec_q.pop(0)[2]()
-
-        def ensure(key):
-            while key not in ready_ops:
-                if any(e[1] == key for e in vec_q):
-                    vec_q.pop(0)[2]()
-                else:
-                    prep_q.pop(0)[1]()
-
-        def fill(s):
-            if prep_q and prep_q[0][0] <= s:
-                prep_q.pop(0)[1]()
-            elif mean_q and mean_q[0][0] <= s:
-                mean_q.pop(0)[1]()
-
-        def push_mean(ready, n, b, gsum):
+        def queue_mean(first_step, n, b, gsum):
             which, hn = n // 2, n % 2
 
             def run():
                 m_ps = psum.tile([P, 512], F32, name="m_ps", tag="m_ps", bufs=2)
-                nc.tensor.matmul(out=m_ps[:], lhsT=bdiag[:], rhs=gsum[:].rearrange("p h d -> p (h d)"), start=True, stop=True)
-                mean_sb = work.tile([P, HB, HS], F32, name="mean_sb", tag="mean_sb")
+                nc.tensor.matmul(
+                    out=m_ps[:], lhsT=same_group[:], rhs=gsum[:].rearrange("p h d -> p (h d)"), start=True, stop=True
+                )
+                mean_sb = work.tile([P, HB, HS], F32, name="mean_sb", tag="mean_sb", bufs=4)
                 nc.scalar.mul(out=mean_sb[:].rearrange("p h d -> p (h d)"), in_=m_ps[:], mul=1.0 / 32.0)
                 nc.sync.dma_start(
                     out=outs[which][b, HB * hn : HB * (hn + 1), :, 32, :].rearrange("h g d -> g h d"),
-                    in_=mean_sb[0:P:8, :, :],
+                    in_=mean_sb[0:P:GP, :, :],
                 )
 
-            mean_q.append([ready, run])
+            mean_q.append([first_step, run])
+
+        def queue_vector_sum(first_step, n, b, o, gsum):
+            def run(step):
+                nc.vector.tensor_reduce(out=gsum[:], in_=o[:].rearrange("p h r d -> p h d r"), axis=AX.X, op=ALU.add)
+                queue_mean(step + 1, n, b, gsum)
+
+            sum_q.append([first_step, run])
 
         live = {}
-        tree_q = []
 
-        def vector_tree(n, b, o, gsum):
-            def run():
-                nc.vector.tensor_reduce(out=gsum[:], in_=o[:].rearrange("p h r d -> p h d r"), axis=AX.X, op=ALU.add)
-                push_mean(state["step"] + 1, n, b, gsum)
-
-            return run
-
-        def step(k, j):
+        def write_step(k, j):
             n, b = UNITS[k]
             which, hn = n // 2, n % 2
             rope = which < 2
-            s = RL * k + j
-            state["step"] = s
-            ensure(("x", b, j))
-            ensure(("w", n))
+            step = RL * k + j
+            while ("x", b, j) not in quantised or ("w", n) not in quantised:
+                write_quantiser()
             wc, ws = wcodes[n]
             if j == 0:
                 live["o"] = opool.tile([P, HB, RL, HS], F32, name="o", tag="o")
@@ -245,8 +219,11 @@ def tile_causalselfattention2_pa_kernel(tc, x, w_attn, freqs_cos, freqs_sin, out
                     start=(g == 0),
                     stop=(g == KP - 1),
                 )
-            if rope and j in SLOTS:
-                fill(s)
+            if rope:
+                if prep_q and prep_q[0][0] <= step:
+                    prep_q.pop(0)[1](step)
+                elif mean_q and mean_q[0][0] <= step:
+                    mean_q.pop(0)[1]()
             ps_hd = ps[:].rearrange("p (h d) -> p h d", h=HB)
             if rope:
                 if j % 2 == 0:
@@ -283,12 +260,13 @@ def tile_causalselfattention2_pa_kernel(tc, x, w_attn, freqs_cos, freqs_sin, out
                     else:
                         dst = gsum[:]
                     nc.vector.tensor_tensor(out=dst, in0=ps_hd, in1=prev, op=ALU.add)
-            run_vec(s)
-            while tree_q and tree_q[0][0] <= s:
-                tree_q.pop(0)[1]()
+            while quant_q and quant_q[0][0] <= step:
+                write_quantiser()
+            while sum_q and sum_q[0][0] <= step:
+                sum_q.pop(0)[1](step)
             if j < RL - 1:
                 return
-            if rope and (n, b) not in VTREE:
+            if rope and (n, b) not in VECTOR_SUMS:
                 half = work.tile([P, HB, 2, HS], F32, name="half", tag="half")
                 nc.gpsimd.tensor_tensor(out=half[:], in0=o[:, :, 0:2, :], in1=o[:, :, 2:4, :], op=ALU.add)
                 nc.gpsimd.tensor_tensor(out=gsum[:], in0=half[:, :, 0, :], in1=half[:, :, 1, :], op=ALU.add)
@@ -297,28 +275,29 @@ def tile_causalselfattention2_pa_kernel(tc, x, w_attn, freqs_cos, freqs_sin, out
                     out=outs[which][b, HB * hn + h, :, 0:32, :].rearrange("g (rh rl) d -> g rh (rl d)", rl=RL),
                     in_=o[:, h, :, :].rearrange("p rl d -> p (rl d)"),
                 )
-            if rope and (n, b) in VTREE:
-                tree_q.append([s + GLAG, vector_tree(n, b, o, gsum)])
+            if rope and (n, b) in VECTOR_SUMS:
+                queue_vector_sum(step + VECTOR_SUM_BEHIND, n, b, o, gsum)
             else:
-                push_mean(s + (MLAG if rope else 1), n, b, gsum)
+                queue_mean(step + (MEAN_BEHIND if rope else 1), n, b, gsum)
 
         for t in range(4):
-            tile_prep("w", blocks[0], t, True)
-            run_vec(0)
-        tile_prep("x", 0, 0, False)
-        tile_prep("x", 0, 1, False)
-        prep_q.append([0, prep_run("x", 0, (2,))])
-        prep_q.append([0, prep_run("x", 0, (3,))])
-        prep_q.append([0, prep_run("x", 1, (0, 1, 2, 3))])
+            prepare_tile("w", blocks[0], t, 0)
+            write_quantiser()
+        prepare_tile("x", 0, 0, 0)
+        prepare_tile("x", 0, 1, 0)
+        prep_q.append([0, lambda step: prepare_tile("x", 0, 2, step)])
+        prep_q.append([0, lambda step: prepare_tile("x", 0, 3, step)])
+        prep_q.append([0, lambda step: prepare_block("x", 1, step)])
+
+        def queue_block(n):
+            first_use = RL * min(k for k in range(len(UNITS)) if UNITS[k][0] == n)
+            prep_q.append([max(0, first_use - PREP_AHEAD), lambda step: prepare_block("w", n, step)])
+
         for n in blocks[1:]:
-            need = RL * min(k for k in range(len(UNITS)) if UNITS[k][0] == n)
-            prep_q.append([max(0, need - AHEAD), prep_run("w", n, (0, 1, 2, 3))])
+            queue_block(n)
 
         for k in range(len(UNITS)):
             for j in range(RL):
-                step(k, j)
-        while tree_q or mean_q:
-            if tree_q:
-                tree_q.pop(0)[1]()
-            else:
-                mean_q.pop(0)[1]()
+                write_step(k, j)
+        while mean_q:
+            mean_q.pop(0)[1]()

@@ -23,6 +23,7 @@ GP = 8
 
 UNITS = ((0, 0), (0, 1), (4, 0), (2, 0), (2, 1), (4, 1), (1, 0), (1, 1), (3, 0), (3, 1), (5, 0), (5, 1))
 VECTOR_SUMS = ((2, 0), (1, 0), (3, 0))
+TENSOR_SUMS = ((1, 1), (3, 1))
 PREP_AHEAD = 7
 QUANT_BEHIND = 2
 VECTOR_SUM_BEHIND = 4
@@ -83,15 +84,11 @@ def tile_causalselfattention2_pa_kernel(tc, x, w_attn, freqs_cos, freqs_sin, out
         same_group = const.tile([P, P], F32, name="bdiag")
         masks.make_block_diagonal(nc, same_group[:], GP)
 
-        ctab = const.tile([P, RL, HS], F32, name="ctab")
-        stab = const.tile([P, RL, HS], F32, name="stab")
-        nc.vector.tensor_copy(
-            out=ctab[:].rearrange("p j (i e) -> p j i e", e=2),
-            in_=cos_sb[:].unsqueeze(3).to_broadcast([P, RL, 32, 2]),
-        )
-        stab_v = stab[:].rearrange("p j (i e) -> p j i e", e=2)
-        nc.vector.tensor_scalar_mul(out=stab_v[:, :, :, 0], in0=sin_sb[:], scalar1=-1.0)
-        nc.vector.tensor_copy(out=stab_v[:, :, :, 1], in_=sin_sb[:])
+        tab = const.tile([P, RL, 2, HS], F32, name="tab")
+        tab_v = tab[:].rearrange("p j s (i e) -> p j s i e", e=2)
+        nc.vector.tensor_copy(out=tab_v[:, :, 0, :, :], in_=cos_sb[:].unsqueeze(3).to_broadcast([P, RL, 32, 2]))
+        nc.vector.tensor_copy(out=tab_v[:, :, 1, :, 0], in_=sin_sb[:])
+        nc.vector.tensor_scalar_mul(out=tab_v[:, :, 1, :, 1], in0=sin_sb[:], scalar1=-1.0)
 
         xc = {}
         xs = {}
@@ -186,6 +183,28 @@ def tile_causalselfattention2_pa_kernel(tc, x, w_attn, freqs_cos, freqs_sin, out
 
             mean_q.append([first_step, run])
 
+        def queue_mean_of_rows(first_step, n, b, o):
+            which, hn = n // 2, n % 2
+
+            def run():
+                m_ps = psum.tile([P, 512], F32, name="m_ps", tag="m_ps", bufs=2)
+                for jj in range(RL):
+                    nc.tensor.matmul(
+                        out=m_ps[:].rearrange("p (h d) -> p h d", h=HB),
+                        lhsT=same_group[:],
+                        rhs=o[:, :, jj, :],
+                        start=(jj == 0),
+                        stop=(jj == RL - 1),
+                    )
+                mean_sb = work.tile([P, HB, HS], F32, name="mean_sb", tag="mean_sb", bufs=4)
+                nc.scalar.mul(out=mean_sb[:].rearrange("p h d -> p (h d)"), in_=m_ps[:], mul=1.0 / 32.0)
+                nc.sync.dma_start(
+                    out=outs[which][b, HB * hn : HB * (hn + 1), :, 32, :].rearrange("h g d -> g h d"),
+                    in_=mean_sb[0:P:GP, :, :],
+                )
+
+            mean_q.append([first_step, run])
+
         def queue_vector_sum(first_step, n, b, o, gsum):
             def run(step):
                 nc.vector.tensor_reduce(out=gsum[:], in_=o[:].rearrange("p h r d -> p h d r"), axis=AX.X, op=ALU.add)
@@ -227,26 +246,29 @@ def tile_causalselfattention2_pa_kernel(tc, x, w_attn, freqs_cos, freqs_sin, out
             ps_hd = ps[:].rearrange("p (h d) -> p h d", h=HB)
             if rope:
                 if j % 2 == 0:
-                    live["m1"] = mpool.tile([P, HB, 2, HS], F32, name="m1", tag="m1")
-                    live["m2"] = mpool.tile([P, HB, 2, HS], F32, name="m2", tag="m2")
-                m1 = live["m1"]
-                m2 = live["m2"]
+                    live["m"] = mpool.tile([P, 2, HB, 2, HS], F32, name="m", tag="m")
+                m = live["m"]
                 nc.vector.tensor_tensor(
-                    out=m1[:, :, j % 2, :],
-                    in0=ps_hd,
-                    in1=ctab[:, j, :].unsqueeze(1).to_broadcast([P, HB, HS]),
+                    out=m[:, :, :, j % 2, :],
+                    in0=ps_hd.unsqueeze(1).to_broadcast([P, 2, HB, HS]),
+                    in1=tab[:, j, :, :].unsqueeze(2).to_broadcast([P, 2, HB, HS]),
                     op=ALU.mult,
                 )
-                nc.vector.tensor_tensor(
-                    out=m2[:, :, j % 2, :].rearrange("p h (i e) -> p h i e", e=2),
-                    in0=ps[:].rearrange("p (h i e) -> p h i e", h=HB, e=2)[:, :, :, ::-1],
-                    in1=stab[:, j, :].rearrange("p (i e) -> p i e", e=2).unsqueeze(1).to_broadcast([P, HB, 32, 2]),
-                    op=ALU.mult,
-                )
+                o_flat = o[:].rearrange("p h r d -> p h (r d)")
+                m_flat = m[:].rearrange("p s h r d -> p s h (r d)")
                 if k == 0:
-                    nc.gpsimd.tensor_tensor(out=o[:, :, j, :], in0=m1[:, :, j % 2, :], in1=m2[:, :, j % 2, :], op=ALU.add)
-                elif j % 2 == 1:
-                    nc.gpsimd.tensor_tensor(out=o[:, :, j - 1 : j + 1, :], in0=m1[:], in1=m2[:], op=ALU.add)
+                    o_cols = slice(HS * j, HS * (j + 1))
+                    m_cols = slice(HS * (j % 2), HS * (j % 2 + 1))
+                else:
+                    o_cols = slice(HS * (j - 1), HS * (j + 1))
+                    m_cols = slice(0, 2 * HS)
+                if k == 0 or j % 2 == 1:
+                    nc.gpsimd.tensor_tensor(
+                        out=o_flat[:, :, o_cols].rearrange("p h (c e) -> p h c e", e=2),
+                        in0=m_flat[:, 0, :, m_cols].rearrange("p h (c e) -> p h c e", e=2),
+                        in1=m_flat[:, 1, :, m_cols].rearrange("p h (c e) -> p h c e", e=2)[:, :, :, ::-1],
+                        op=ALU.add,
+                    )
             else:
                 nc.scalar.copy(out=o[:, :, j, :], in_=ps_hd)
                 if j == 0:
@@ -266,7 +288,7 @@ def tile_causalselfattention2_pa_kernel(tc, x, w_attn, freqs_cos, freqs_sin, out
                 sum_q.pop(0)[1](step)
             if j < RL - 1:
                 return
-            if rope and (n, b) not in VECTOR_SUMS:
+            if rope and (n, b) not in VECTOR_SUMS and (n, b) not in TENSOR_SUMS:
                 half = work.tile([P, HB, 2, HS], F32, name="half", tag="half")
                 nc.gpsimd.tensor_tensor(out=half[:], in0=o[:, :, 0:2, :], in1=o[:, :, 2:4, :], op=ALU.add)
                 nc.gpsimd.tensor_tensor(out=gsum[:], in0=half[:, :, 0, :], in1=half[:, :, 1, :], op=ALU.add)
@@ -277,6 +299,8 @@ def tile_causalselfattention2_pa_kernel(tc, x, w_attn, freqs_cos, freqs_sin, out
                 )
             if rope and (n, b) in VECTOR_SUMS:
                 queue_vector_sum(step + VECTOR_SUM_BEHIND, n, b, o, gsum)
+            elif (n, b) in TENSOR_SUMS:
+                queue_mean_of_rows(step + MEAN_BEHIND, n, b, o)
             else:
                 queue_mean(step + (MEAN_BEHIND if rope else 1), n, b, gsum)
 

@@ -21,13 +21,28 @@ HB = 8
 HS = 64
 GP = 8
 
-UNITS = ((0, 0), (0, 1), (4, 0), (2, 0), (2, 1), (4, 1), (1, 0), (1, 1), (3, 0), (3, 1), (5, 0), (5, 1))
+UNITS = ((0, 0), (0, 1), (2, 0), (2, 1), (1, 0), (1, 1), (3, 0), (3, 1), (4, 0), (4, 1), (5, 0), (5, 1))
 VECTOR_SUMS = ((2, 0), (1, 0), (3, 0))
 TENSOR_SUMS = ((1, 1), (3, 1))
-PREP_AHEAD = 7
-QUANT_BEHIND = 2
-VECTOR_SUM_BEHIND = 4
-MEAN_BEHIND = 8
+PREP_AHEAD = 10
+QUANT_BEHIND = 3
+VECTOR_SUM_BEHIND = 6
+MEAN_BEHIND = 12
+
+V_START = 4
+V_EVERY = 2
+
+
+def step_order():
+    rope_steps = [(k, j) for k in range(len(UNITS)) if UNITS[k][0] < 4 for j in range(RL)]
+    v_steps = [(k, j) for k in range(len(UNITS)) if UNITS[k][0] >= 4 for j in range(RL)]
+    steps = []
+    for count, rope_step in enumerate(rope_steps):
+        steps.append(rope_step)
+        if count + 1 > V_START and (count + 1) % V_EVERY == 0 and v_steps:
+            steps.append(v_steps.pop(0))
+    steps.extend(v_steps)
+    return steps
 
 
 def tile_causalselfattention2_pa_kernel(tc, x, w_attn, freqs_cos, freqs_sin, out_0, out_1, out_2):
@@ -44,10 +59,11 @@ def tile_causalselfattention2_pa_kernel(tc, x, w_attn, freqs_cos, freqs_sin, out
         work = ctx.enter_context(tc.tile_pool(name="work", bufs=2))
         psum = ctx.enter_context(tc.psum_pool(name="psum", bufs=1))
 
+        steps = step_order()
         blocks = []
-        for n, b in UNITS:
-            if n not in blocks:
-                blocks.append(n)
+        for k, j in steps:
+            if UNITS[k][0] not in blocks:
+                blocks.append(UNITS[k][0])
 
         cos_sb = const.tile([P, RL, 32], BF16, name="cos_sb")
         sin_sb = const.tile([P, RL, 32], BF16, name="sin_sb")
@@ -212,15 +228,18 @@ def tile_causalselfattention2_pa_kernel(tc, x, w_attn, freqs_cos, freqs_sin, out
 
             sum_q.append([first_step, run])
 
-        live = {}
+        live_of = {}
 
-        def write_step(k, j):
+        def write_step(k, j, step):
             n, b = UNITS[k]
             which, hn = n // 2, n % 2
             rope = which < 2
-            step = RL * k + j
+            live = live_of.setdefault(k, {})
             while ("x", b, j) not in quantised or ("w", n) not in quantised:
-                write_quantiser()
+                if quant_q:
+                    write_quantiser()
+                else:
+                    prep_q.pop(0)[1](step)
             wc, ws = wcodes[n]
             if j == 0:
                 live["o"] = opool.tile([P, HB, RL, HS], F32, name="o", tag="o")
@@ -238,11 +257,10 @@ def tile_causalselfattention2_pa_kernel(tc, x, w_attn, freqs_cos, freqs_sin, out
                     start=(g == 0),
                     stop=(g == KP - 1),
                 )
-            if rope:
-                if prep_q and prep_q[0][0] <= step:
-                    prep_q.pop(0)[1](step)
-                elif mean_q and mean_q[0][0] <= step:
-                    mean_q.pop(0)[1]()
+            if prep_q and prep_q[0][0] <= step:
+                prep_q.pop(0)[1](step)
+            elif mean_q and mean_q[0][0] <= step:
+                mean_q.pop(0)[1]()
             ps_hd = ps[:].rearrange("p (h d) -> p h d", h=HB)
             if rope:
                 if j % 2 == 0:
@@ -314,14 +332,13 @@ def tile_causalselfattention2_pa_kernel(tc, x, w_attn, freqs_cos, freqs_sin, out
         prep_q.append([0, lambda step: prepare_block("x", 1, step)])
 
         def queue_block(n):
-            first_use = RL * min(k for k in range(len(UNITS)) if UNITS[k][0] == n)
+            first_use = min(at for at in range(len(steps)) if UNITS[steps[at][0]][0] == n)
             prep_q.append([max(0, first_use - PREP_AHEAD), lambda step: prepare_block("w", n, step)])
 
         for n in blocks[1:]:
             queue_block(n)
 
-        for k in range(len(UNITS)):
-            for j in range(RL):
-                write_step(k, j)
+        for at in range(len(steps)):
+            write_step(steps[at][0], steps[at][1], at)
         while mean_q:
             mean_q.pop(0)[1]()

@@ -23,7 +23,7 @@ GP = 8
 
 UNITS = ((0, 0), (0, 1), (2, 0), (2, 1), (1, 0), (1, 1), (3, 0), (3, 1), (4, 0), (4, 1), (5, 0), (5, 1))
 VECTOR_SUMS = ((2, 0), (1, 0), (3, 0))
-TENSOR_SUMS = ((1, 1), (3, 1))
+TENSOR_SUMS = ()
 PREP_AHEAD = 10
 QUANT_BEHIND = 3
 VECTOR_SUM_BEHIND = 6

@@ -23,7 +23,7 @@ GP = 8
 
 UNITS = ((0, 0), (0, 1), (2, 0), (2, 1), (1, 0), (1, 1), (3, 0), (3, 1), (4, 0), (4, 1), (5, 0), (5, 1))
 VECTOR_SUMS = ((2, 0), (1, 0), (3, 0))
-TENSOR_SUMS = ()
+TENSOR_SUMS = ((3, 1),)
 PREP_AHEAD = 10
 QUANT_BEHIND = 3
 VECTOR_SUM_BEHIND = 6

@@ -29,6 +29,8 @@ QUANT_BEHIND = 3
 VECTOR_SUM_BEHIND = 6
 MEAN_BEHIND = 12
 
+WARM_UP = 5
+
 V_START = 4
 V_EVERY = 2
 
@@ -94,6 +96,12 @@ def tile_causalselfattention2_pa_kernel(tc, x, w_attn, freqs_cos, freqs_sin, out
         nc.sync.dma_start(out=x1_sb[:], in_=x_rows[1])
         for n in blocks[1:]:
             nc.sync.dma_start(out=w_sb[n][:], in_=w_rows(n))
+
+        zeros = const.tile([P, 512], BF16, name="zeros")
+        nc.vector.memset(zeros[:], 0.0)
+        warm_ps = psum.tile([P, 512], F32, name="warm_ps", tag="ps", bufs=4)
+        for i in range(WARM_UP):
+            nc.tensor.matmul(out=warm_ps[:], lhsT=zeros[:, 0:P], rhs=zeros[:], start=True, stop=True)
 
         ident = const.tile([P, P], F32, name="ident")
         masks.make_identity(nc, ident[:])

from contextlib import ExitStack

import concourse.masks as masks
import concourse.mybir as mybir

FLOPS = 2 * 1024 * 3072 * 1024

F32 = mybir.dt.float32
BF16 = mybir.dt.bfloat16
U32 = mybir.dt.uint32
U8 = mybir.dt.uint8
FP8X4 = mybir.dt.float8_e5m2_x4
ALU = mybir.AluOpType
AX = mybir.AxisListType

P = 128
NB = 2
RL = 4
KP = 2
HB = 8
HS = 64
GP = 8

UNITS = ((0, 0), (0, 1), (2, 0), (2, 1), (1, 0), (1, 1), (3, 0), (3, 1), (4, 0), (4, 1), (5, 0), (5, 1))
VECTOR_SUMS = ((2, 0), (1, 0), (3, 0))
TENSOR_SUMS = ((3, 1),)
PREP_AHEAD = 10
QUANT_BEHIND = 3
VECTOR_SUM_BEHIND = 6
MEAN_BEHIND = 12

WARM_UP = 5

V_START = 4
V_EVERY = 2


def step_order():
    rope_steps = [(k, j) for k in range(len(UNITS)) if UNITS[k][0] < 4 for j in range(RL)]
    v_steps = [(k, j) for k in range(len(UNITS)) if UNITS[k][0] >= 4 for j in range(RL)]
    steps = []
    for count, rope_step in enumerate(rope_steps):
        steps.append(rope_step)
        if count + 1 > V_START and (count + 1) % V_EVERY == 0 and v_steps:
            steps.append(v_steps.pop(0))
    steps.extend(v_steps)
    return steps


def tile_causalselfattention2_pa_kernel(tc, x, w_attn, freqs_cos, freqs_sin, out_0, out_1, out_2):
    nc = tc.nc
    outs = (out_0, out_1, out_2)

    with ExitStack() as ctx:
        const = ctx.enter_context(tc.tile_pool(name="const", bufs=1))
        wraw = ctx.enter_context(tc.tile_pool(name="wraw", bufs=5))
        stage = ctx.enter_context(tc.tile_pool(name="stage", bufs=3))
        wq = ctx.enter_context(tc.tile_pool(name="wq", bufs=4))
        opool = ctx.enter_context(tc.tile_pool(name="opool", bufs=5))
        mpool = ctx.enter_context(tc.tile_pool(name="mpool", bufs=4))
        work = ctx.enter_context(tc.tile_pool(name="work", bufs=2))
        psum = ctx.enter_context(tc.psum_pool(name="psum", bufs=1))

        steps = step_order()
        blocks = []
        for k, j in steps:
            if UNITS[k][0] not in blocks:
                blocks.append(UNITS[k][0])

        cos_sb = const.tile([P, RL, 32], BF16, name="cos_sb")
        sin_sb = const.tile([P, RL, 32], BF16, name="sin_sb")
        nc.scalar.dma_start(out=cos_sb[:], in_=freqs_cos.rearrange("(p j) i -> p j i", j=RL))
        nc.scalar.dma_start(out=sin_sb[:], in_=freqs_sin.rearrange("(p j) i -> p j i", j=RL))

        rows_of = {}
        for j in range(RL):
            rows_of[("x", 0, j)] = const.tile([P, 1024], BF16, name="x0_%d" % j)
            rows_of[("w", blocks[0], j)] = const.tile([P, 1024], BF16, name="w0_%d" % j)
        x1_sb = const.tile([P, RL, 1024], BF16, name="x1_sb")
        for j in range(RL):
            rows_of[("x", 1, j)] = x1_sb[:, j, :]
        w_sb = {}
        for n in blocks[1:]:
            w_sb[n] = wraw.tile([P, 4, 1024], BF16, name="w_sb", tag="w_sb")
            for t in range(4):
                rows_of[("w", n, t)] = w_sb[n][:, t, :]

        def w_rows(n):
            return w_attn[512 * n : 512 * (n + 1), :].rearrange("(t p) k -> p t k", p=P)

        for t in range(4):
            nc.sync.dma_start(out=rows_of[("w", blocks[0], t)][:], in_=w_rows(blocks[0])[:, t, :])
        x_rows = x.rearrange("b (p j) k -> b p j k", j=RL)
        for j in range(RL):
            nc.sync.dma_start(out=rows_of[("x", 0, j)][:], in_=x_rows[0, :, j, :])
        nc.sync.dma_start(out=x1_sb[:], in_=x_rows[1])
        for n in blocks[1:]:
            nc.sync.dma_start(out=w_sb[n][:], in_=w_rows(n))

        zeros = const.tile([P, 512], BF16, name="zeros")
        nc.vector.memset(zeros[:], 0.0)
        warm_ps = psum.tile([P, 512], F32, name="warm_ps", tag="ps", bufs=4)
        for i in range(WARM_UP):
            nc.tensor.matmul(out=warm_ps[:], lhsT=zeros[:, 0:P], rhs=zeros[:], start=True, stop=True)

        ident = const.tile([P, P], F32, name="ident")
        masks.make_identity(nc, ident[:])
        same_group = const.tile([P, P], F32, name="bdiag")
        masks.make_block_diagonal(nc, same_group[:], GP)

        tab = const.tile([P, RL, 2, HS], F32, name="tab")
        tab_v = tab[:].rearrange("p j s (i e) -> p j s i e", e=2)
        nc.vector.tensor_copy(out=tab_v[:, :, 0, :, :], in_=cos_sb[:].unsqueeze(3).to_broadcast([P, RL, 32, 2]))
        nc.vector.tensor_copy(out=tab_v[:, :, 1, :, 0], in_=sin_sb[:])
        nc.vector.tensor_scalar_mul(out=tab_v[:, :, 1, :, 1], in0=sin_sb[:], scalar1=-1.0)

        xc = {}
        xs = {}
        xc1 = const.tile([P, KP, 512], U32, name="xc1", align_bytes=64)
        xs1 = const.tile([P, KP, 512], U8, name="xs1", align_bytes=64)
        for j in range(RL):
            xc[(0, j)] = const.tile([P, KP, P], U32, name="xc0_%d" % j, align_bytes=64)
            xs[(0, j)] = const.tile([P, KP, P], U8, name="xs0_%d" % j, align_bytes=64)
            xc[(1, j)] = xc1[:, :, P * j : P * (j + 1)]
            xs[(1, j)] = xs1[:, :, P * j : P * (j + 1)]
        wcodes = {}

        prep_q = []
        mean_q = []
        quant_q = []
        sum_q = []
        quantised = set()

        def quantise(grouped, codes, scales):
            nc.vector.quantize_mx(
                out=codes[:].rearrange("p g c -> p (g c)").bitcast(FP8X4),
                scales=scales[:].rearrange("p g c -> p (g c)"),
                in_=grouped[:].rearrange("p g t r j -> p (g t r j)"),
            )

        def quantise_columns(grouped, codes, scales):
            for g in range(KP):
                nc.vector.quantize_mx(
                    out=codes[:, g, :].bitcast(FP8X4),
                    scales=scales[:, g, :],
                    in_=grouped[:, g].rearrange("p t r j -> p (t r j)"),
                )

        def transpose_rows(rows, grouped, slot):
            words = rows.bitcast(F32)
            tp = psum.tile([P, KP, 2, P], F32, name="tp", tag="tp", bufs=2)
            for g in range(KP):
                for u in range(2):
                    nc.tensor.transpose(tp[:, g, u, :], words[:, 256 * g + u : 256 * (g + 1) : 2], ident[:])
            nc.scalar.copy(out=grouped[:].bitcast(F32)[:, :, slot, :, :], in_=tp[:].rearrange("p g u r -> p g r u"))

        def new_w_codes(n):
            wc = wq.tile([P, KP, 512], U32, name="wc", tag="wc", align_bytes=64)
            ws = wq.tile([P, KP, 512], U8, name="ws", tag="ws", align_bytes=64)
            wcodes[n] = (wc, ws)

        def prepare_tile(operand, index, t, step):
            if operand == "w" and t == 0:
                new_w_codes(index)
            grouped = stage.tile([P, KP, 1, P, 4], BF16, name="grouped1", tag="grouped1", bufs=4, align_bytes=64)
            transpose_rows(rows_of[(operand, index, t)], grouped, 0)
            if operand == "x":
                quant_q.append([step + 1, [("x", 0, t)], lambda: quantise(grouped, xc[(0, t)], xs[(0, t)])])
            else:
                cols = slice(P * t, P * (t + 1))
                wc, ws = wcodes[index]
                done = [("w", index)] if t == 3 else []
                quant_q.append([step, done, lambda: quantise_columns(grouped, wc[:, :, cols], ws[:, :, cols])])

        def prepare_block(operand, index, step):
            if operand == "w":
                new_w_codes(index)
            grouped = stage.tile([P, KP, 4, P, 4], BF16, name="grouped", tag="grouped", align_bytes=64)
            for t in range(4):
                transpose_rows(rows_of[(operand, index, t)], grouped, t)
            if operand == "x":
                quant_q.append([step + 1, [("x", 1, j) for j in range(RL)], lambda: quantise(grouped, xc1, xs1)])
            else:
                wc, ws = wcodes[index]
                quant_q.append([step + QUANT_BEHIND, [("w", index)], lambda: quantise(grouped, wc, ws)])

        def write_quantiser():
            entry = quant_q.pop(0)
            entry[2]()
            for operand in entry[1]:
                quantised.add(operand)

        def queue_mean(first_step, n, b, gsum):
            which, hn = n // 2, n % 2

            def run():
                m_ps = psum.tile([P, 512], F32, name="m_ps", tag="m_ps", bufs=2)
                nc.tensor.matmul(
                    out=m_ps[:], lhsT=same_group[:], rhs=gsum[:].rearrange("p h d -> p (h d)"), start=True, stop=True
                )
                mean_sb = work.tile([P, HB, HS], F32, name="mean_sb", tag="mean_sb", bufs=4)
                nc.scalar.mul(out=mean_sb[:].rearrange("p h d -> p (h d)"), in_=m_ps[:], mul=1.0 / 32.0)
                nc.sync.dma_start(
                    out=outs[which][b, HB * hn : HB * (hn + 1), :, 32, :].rearrange("h g d -> g h d"),
                    in_=mean_sb[0:P:GP, :, :],
                )

            mean_q.append([first_step, run])

        def queue_mean_of_rows(first_step, n, b, o):
            which, hn = n // 2, n % 2

            def run():
                m_ps = psum.tile([P, 512], F32, name="m_ps", tag="m_ps", bufs=2)
                for jj in range(RL):
                    nc.tensor.matmul(
                        out=m_ps[:].rearrange("p (h d) -> p h d", h=HB),
                        lhsT=same_group[:],
                        rhs=o[:, :, jj, :],
                        start=(jj == 0),
                        stop=(jj == RL - 1),
                    )
                mean_sb = work.tile([P, HB, HS], F32, name="mean_sb", tag="mean_sb", bufs=4)
                nc.scalar.mul(out=mean_sb[:].rearrange("p h d -> p (h d)"), in_=m_ps[:], mul=1.0 / 32.0)
                nc.sync.dma_start(
                    out=outs[which][b, HB * hn : HB * (hn + 1), :, 32, :].rearrange("h g d -> g h d"),
                    in_=mean_sb[0:P:GP, :, :],
                )

            mean_q.append([first_step, run])

        def queue_vector_sum(first_step, n, b, o, gsum):
            def run(step):
                nc.vector.tensor_reduce(out=gsum[:], in_=o[:].rearrange("p h r d -> p h d r"), axis=AX.X, op=ALU.add)
                queue_mean(step + 1, n, b, gsum)

            sum_q.append([first_step, run])

        live_of = {}

        def write_step(k, j, step):
            n, b = UNITS[k]
            which, hn = n // 2, n % 2
            rope = which < 2
            live = live_of.setdefault(k, {})
            while ("x", b, j) not in quantised or ("w", n) not in quantised:
                if quant_q:
                    write_quantiser()
                else:
                    prep_q.pop(0)[1](step)
            wc, ws = wcodes[n]
            if j == 0:
                live["o"] = opool.tile([P, HB, RL, HS], F32, name="o", tag="o")
                live["gsum"] = work.tile([P, HB, HS], F32, name="gsum", tag="gsum", bufs=4)
            o = live["o"]
            gsum = live["gsum"]
            ps = psum.tile([P, 512], F32, name="ps", tag="ps", bufs=4)
            for g in range(KP):
                nc.tensor.matmul_mx(
                    out=ps[:],
                    lhsT=xc[(b, j)][:, g, :].bitcast(FP8X4),
                    lhsT_scale=xs[(b, j)][:, g, :],
                    rhs=wc[:, g, :].bitcast(FP8X4),
                    rhs_scale=ws[:, g, :],
                    start=(g == 0),
                    stop=(g == KP - 1),
                )
            if prep_q and prep_q[0][0] <= step:
                prep_q.pop(0)[1](step)
            elif mean_q and mean_q[0][0] <= step:
                mean_q.pop(0)[1]()
            ps_hd = ps[:].rearrange("p (h d) -> p h d", h=HB)
            if rope:
                if j % 2 == 0:
                    live["m"] = mpool.tile([P, 2, HB, 2, HS], F32, name="m", tag="m")
                m = live["m"]
                nc.vector.tensor_tensor(
                    out=m[:, :, :, j % 2, :],
                    in0=ps_hd.unsqueeze(1).to_broadcast([P, 2, HB, HS]),
                    in1=tab[:, j, :, :].unsqueeze(2).to_broadcast([P, 2, HB, HS]),
                    op=ALU.mult,
                )
                o_flat = o[:].rearrange("p h r d -> p h (r d)")
                m_flat = m[:].rearrange("p s h r d -> p s h (r d)")
                if k == 0:
                    o_cols = slice(HS * j, HS * (j + 1))
                    m_cols = slice(HS * (j % 2), HS * (j % 2 + 1))
                else:
                    o_cols = slice(HS * (j - 1), HS * (j + 1))
                    m_cols = slice(0, 2 * HS)
                if k == 0 or j % 2 == 1:
                    nc.gpsimd.tensor_tensor(
                        out=o_flat[:, :, o_cols].rearrange("p h (c e) -> p h c e", e=2),
                        in0=m_flat[:, 0, :, m_cols].rearrange("p h (c e) -> p h c e", e=2),
                        in1=m_flat[:, 1, :, m_cols].rearrange("p h (c e) -> p h c e", e=2)[:, :, :, ::-1],
                        op=ALU.add,
                    )
            else:
                nc.scalar.copy(out=o[:, :, j, :], in_=ps_hd)
                if j == 0:
                    live["acc"] = work.tile([P, HB, HS], F32, name="acc", tag="acc", bufs=3)
                    nc.scalar.copy(out=live["acc"][:], in_=ps_hd)
                else:
                    prev = live["acc"][:]
                    if j < RL - 1:
                        live["acc"] = work.tile([P, HB, HS], F32, name="acc", tag="acc", bufs=3)
                        dst = live["acc"][:]
                    else:
                        dst = gsum[:]
                    nc.vector.tensor_tensor(out=dst, in0=ps_hd, in1=prev, op=ALU.add)
            while quant_q and quant_q[0][0] <= step:
                write_quantiser()
            while sum_q and sum_q[0][0] <= step:
                sum_q.pop(0)[1](step)
            if j < RL - 1:
                return
            if rope and (n, b) not in VECTOR_SUMS and (n, b) not in TENSOR_SUMS:
                half = work.tile([P, HB, 2, HS], F32, name="half", tag="half")
                nc.gpsimd.tensor_tensor(out=half[:], in0=o[:, :, 0:2, :], in1=o[:, :, 2:4, :], op=ALU.add)
                nc.gpsimd.tensor_tensor(out=gsum[:], in0=half[:, :, 0, :], in1=half[:, :, 1, :], op=ALU.add)
            for h in range(HB):
                nc.sync.dma_start(
                    out=outs[which][b, HB * hn + h, :, 0:32, :].rearrange("g (rh rl) d -> g rh (rl d)", rl=RL),
                    in_=o[:, h, :, :].rearrange("p rl d -> p (rl d)"),
                )
            if rope and (n, b) in VECTOR_SUMS:
                queue_vector_sum(step + VECTOR_SUM_BEHIND, n, b, o, gsum)
            elif (n, b) in TENSOR_SUMS:
                queue_mean_of_rows(step + MEAN_BEHIND, n, b, o)
            else:
                queue_mean(step + (MEAN_BEHIND if rope else 1), n, b, gsum)

        for t in range(4):
            prepare_tile("w", blocks[0], t, 0)
            write_quantiser()
        prepare_tile("x", 0, 0, 0)
        prepare_tile("x", 0, 1, 0)
        prep_q.append([0, lambda step: prepare_tile("x", 0, 2, step)])
        prep_q.append([0, lambda step: prepare_tile("x", 0, 3, step)])
        prep_q.append([0, lambda step: prepare_block("x", 1, step)])

        def queue_block(n):
            first_use = min(at for at in range(len(steps)) if UNITS[steps[at][0]][0] == n)
            prep_q.append([max(0, first_use - PREP_AHEAD), lambda step: prepare_block("w", n, step)])

        for n in blocks[1:]:
            queue_block(n)

        for at in range(len(steps)):
            write_step(steps[at][0], steps[at][1], at)
        while mean_q:
            mean_q.pop(0)[1]()
